import numpy as np
import ml_dtypes


def mxq(x, axis, fmt="e4m3"):
    dtype, down = {"e4m3": (ml_dtypes.float8_e4m3fn, 7), "e5m2": (ml_dtypes.float8_e5m2, 14)}[fmt]
    v = np.moveaxis(np.asarray(x, np.float32).astype(ml_dtypes.bfloat16).astype(np.float64), axis, -1)
    blocks = v.reshape(v.shape[:-1] + (-1, 32))
    amax = np.abs(blocks).max(-1, keepdims=True)
    byte = np.maximum(np.where(amax > 0, np.frexp(amax)[1] - 1 + 127, 0) - down, 1)
    scale = np.exp2(byte - 127.0)
    codes = (blocks / scale).astype(np.float32).astype(dtype).astype(np.float64)
    return np.moveaxis((codes * scale).reshape(v.shape), -1, axis)


WIDE = False


def mx_kscale(k):
    if not WIDE:
        return np.ones(k)
    levels = np.array([10, -10, 5, -5, 0])
    a = np.random.permutation(np.resize(levels, k // 512 * 4)).reshape(k // 512, 4)
    idx = np.arange(k)
    return np.exp2(a[idx // 512, idx % 128 // 32])


BF16 = ml_dtypes.bfloat16


def bf(x):
    return np.asarray(x, np.float32).astype(BF16)


def f64(x):
    return np.asarray(x).astype(np.float64)


B, K, N = 2048, 512, 1024
NACT = 4


def setup_inputs():
    s = mx_kscale(K)
    g = np.tile(np.array([1.0, 1.0, 1.0, 0.5]), N // NACT)
    x = np.random.standard_normal((B, K)) * s
    weight = np.random.uniform(-1.0, 1.0, (N, K)) / np.sqrt(K) * g[:, None] / s[None, :]
    return {"x": bf(x), "weight": bf(weight)}


def reference(x, weight):
    y = mxq(f64(x), 1, "e4m3") @ mxq(f64(weight), 1, "e4m3").T
    rows, cols = y.shape
    y3 = y.reshape(rows, cols // NACT, NACT)
    out = np.stack(
        [y3[..., 0],
         np.cos(y3[..., 1]),
         np.sin(y3[..., 2]),
         np.tan(y3[..., 3])],
        axis=-1,
    )
    return out.reshape(rows, cols)

@@ -1,0 +1,207 @@
+import math
+from contextlib import ExitStack
+
+import concourse.bass as bass
+import concourse.mybir as mybir
+import concourse.tile as tile
+from concourse.masks import make_identity
+
+FLOPS = 2 * 2048 * 512 * 1024
+
+F32 = mybir.dt.float32
+BF16 = mybir.dt.bfloat16
+U32 = mybir.dt.uint32
+U8 = mybir.dt.uint8
+FP8X4 = mybir.dt.float8_e4m3fn_x4
+ACT = mybir.ActivationFunctionType
+MULT = mybir.AluOpType.mult
+
+P = 128
+K = 512
+ROW_TILES = 16
+PAIRS = 8
+BATCHES = 4
+
+
+def tile_mylayerfunc_kernel(tc, x, weight, out):
+    nc = tc.nc
+    with ExitStack() as ctx:
+        keep = ctx.enter_context(tc.tile_pool(name="keep", bufs=1))
+        work = ctx.enter_context(tc.tile_pool(name="work", bufs=2))
+        psum = ctx.enter_context(tc.psum_pool(name="psum", bufs=8))
+
+        half_pi = keep.tile([P, 1], F32, name="half_pi")
+        zero = keep.tile([P, 1], F32, name="zero")
+        nc.vector.memset(zero[:], 0.0)
+        nc.vector.tensor_scalar_add(out=half_pi[:], in0=zero[:], scalar1=math.pi / 2)
+        warm = keep.tile([P, 1], F32, name="warm")
+        nc.scalar.activation(out=warm[:], in_=half_pi[:], func=ACT.Sin)
+        ident = keep.tile([P, P], F32, name="ident")
+        make_identity(nc, ident[:])
+
+        w_raw = keep.tile([P, 2 * 4 * K], BF16, name="w_raw")
+        w_view = weight.rearrange("(h p c) k -> h p (c k)", h=2, p=P, c=4)
+        for h in range(2):
+            nc.sync.dma_start(out=w_raw[:, h * 2048:(h + 1) * 2048], in_=w_view[h])
+        x_raw = keep.tile([P, ROW_TILES * K], BF16, name="x_raw")
+        x_view = x.rearrange("(p r) k -> p (r k)", r=ROW_TILES)
+        for b in range(BATCHES):
+            nc.sync.dma_start(out=x_raw[:, b * 2048:(b + 1) * 2048], in_=x_view[:, b * 2048:(b + 1) * 2048])
+        w_words = w_raw[:].bitcast(F32)
+        x_words = x_raw[:].bitcast(F32)
+
+        w_grp = keep.tile([P, 4096], BF16, name="w_grp", align_bytes=64)
+        x_grp = keep.tile([P, 8192], BF16, name="x_grp", align_bytes=64)
+        w_grp_words = w_grp[:].bitcast(F32)
+        x_grp_words = x_grp[:].bitcast(F32)
+        w_codes = keep.tile([P, 1024], U32, name="w_codes", align_bytes=64)
+        w_scales = keep.tile([P, 1024], U8, name="w_scales", align_bytes=64)
+        x_codes = keep.tile([P, 2048], U32, name="x_codes", align_bytes=64)
+        x_scales = keep.tile([P, 2048], U8, name="x_scales", align_bytes=64)
+
+        def transpose_bank(words, starts, label):
+            bank = psum.tile([P, 512], F32, name=label, tag="bank")
+            halves = bank[:].rearrange("p (u n) -> p u n", u=2)
+            for blk in range(2):
+                for u in range(2):
+                    lo = starts[blk] + u * P
+                    nc.tensor.transpose(halves[:, u, blk * P:(blk + 1) * P], words[:, lo:lo + P], ident[:])
+            return bank
+
+        def leave(on_vector, bank, dst_words):
+            dst = dst_words.rearrange("p (n u) -> p n u", u=2)
+            src = bank[:].rearrange("p (u n) -> p n u", u=2)
+            if on_vector:
+                nc.vector.tensor_copy(out=dst, in_=src)
+            else:
+                nc.scalar.copy(out=dst, in_=src)
+
+        w_banks = [transpose_bank(w_words, [c * 256, 1024 + c * 256], "wt%d" % c) for c in range(4)]
+        for c in range(4):
+            leave(c % 2 == 0, w_banks[c], w_grp_words[:, c * 512:(c + 1) * 512])
+        x_banks = {}
+        for q in range(4):
+            x_banks[q] = transpose_bank(x_words, [2 * q * 256, (2 * q + 1) * 256], "xt%d" % q)
+        for c in range(4):
+            nc.vector.quantize_mx(
+                out=w_codes[:, c * 256:(c + 1) * 256].bitcast(FP8X4),
+                scales=w_scales[:, c * 256:(c + 1) * 256],
+                in_=w_grp[:, c * 1024:(c + 1) * 1024],
+            )
+            leave(c % 2 == 0, x_banks[c], x_grp_words[:, c * 512:(c + 1) * 512])
+        for q in range(4, PAIRS):
+            x_banks[q] = transpose_bank(x_words, [2 * q * 256, (2 * q + 1) * 256], "xt%d" % q)
+
+        def quantise_x(b):
+            nc.vector.quantize_mx(
+                out=x_codes[:, b * 512:(b + 1) * 512].bitcast(FP8X4),
+                scales=x_scales[:, b * 512:(b + 1) * 512],
+                in_=x_grp[:, b * 2048:(b + 1) * 2048],
+            )
+
+        quantise_x(0)
+        leave(True, x_banks[4], x_grp_words[:, 4 * 512:5 * 512])
+        leave(False, x_banks[5], x_grp_words[:, 5 * 512:6 * 512])
+        quantise_x(1)
+        leave(True, x_banks[6], x_grp_words[:, 6 * 512:7 * 512])
+        leave(False, x_banks[7], x_grp_words[:, 7 * 512:8 * 512])
+        quantise_x(2)
+        quantise_x(3)
+
+        def mx_bank(pair, cls):
+            bank = psum.tile([P, 512], F32, name="y%d_%d" % (cls, pair), tag="bank")
+            for t in range(2):
+                r = 2 * pair + t
+                nc.tensor.matmul_mx(
+                    out=bank[:, t * 256:(t + 1) * 256],
+                    lhsT=x_codes[:, r * P:(r + 1) * P].bitcast(FP8X4),
+                    lhsT_scale=x_scales[:, r * P:(r + 1) * P],
+                    rhs=w_codes[:, cls * 256:(cls + 1) * 256].bitcast(FP8X4),
+                    rhs_scale=w_scales[:, cls * 256:(cls + 1) * 256],
+                    start=True,
+                    stop=True,
+                )
+            return bank
+
+        out_view = out.rearrange("(p r) j -> p (r j)", r=ROW_TILES)
+        planes = {}
+
+        def scalar_part(b):
+            cosines = work.tile([P, 2, 512], F32, name="cos3_%d" % b, tag="cos3")
+            sines = work.tile([P, 2, 512], F32, name="sin3_%d" % b, tag="sin3")
+            mags = work.tile([P, 2, 512], F32, name="abs3_%d" % b, tag="abs3")
+            res = work.tile([P, 2, 4, 512], F32, name="res_%d" % b, tag="res", bufs=3)
+            pa = 2 * b
+            pb = 2 * b + 1
+            y3a = mx_bank(pa, 3)
+            y3b = mx_bank(pb, 3)
+            nc.scalar.activation(out=mags[:, 0, :], in_=y3a[:], func=ACT.Abs)
+            nc.scalar.activation(out=sines[:, 1, :], in_=y3a[:], func=ACT.Sin)
+            nc.scalar.activation(out=mags[:, 1, :], in_=y3b[:], func=ACT.Abs)
+            nc.scalar.activation(out=cosines[:, 0, :], in_=mags[:, 0, :], func=ACT.Sin, scale=-1.0, bias=half_pi[:])
+            nc.scalar.activation(out=sines[:, 0, :], in_=y3b[:], func=ACT.Sin)
+            nc.scalar.activation(out=cosines[:, 1, :], in_=mags[:, 1, :], func=ACT.Sin, scale=-1.0, bias=half_pi[:])
+            for pair, slot in ((pa, 1), (pb, 0)):
+                mag1 = work.tile([P, 512], F32, name="abs1_%d" % pair, tag="abs1")
+                y1 = mx_bank(pair, 1)
+                y2 = mx_bank(pair, 2)
+                y0 = mx_bank(pair, 0)
+                nc.scalar.activation(out=mag1[:], in_=y1[:], func=ACT.Abs)
+                nc.scalar.activation(out=res[:, slot, 2, :], in_=y2[:], func=ACT.Sin)
+                nc.scalar.activation(out=res[:, slot, 1, :], in_=mag1[:], func=ACT.Sin, scale=-1.0, bias=half_pi[:])
+                nc.scalar.copy(out=res[:, slot, 0, :], in_=y0[:])
+            planes[b] = res
+            return cosines, sines
+
+        stage = {}
+
+        def interleave(b, step):
+            j = step // 2
+            t = step % 2
+            pair = 2 * b + j
+            slot = 1 - j
+            if t == 0:
+                stage[pair] = work.tile([P, 2048], F32, name="o_%d" % pair, tag="o", bufs=4)
+            o = stage[pair]
+            nc.vector.tensor_copy(
+                out=o[:, t * 1024:(t + 1) * 1024].rearrange("p (i c) -> p i c", c=4),
+                in_=planes[b][:, slot, :, t * 256:(t + 1) * 256].rearrange("p c i -> p i c"),
+            )
+            if t == 1:
+                nc.sync.dma_start(out=out_view[:, pair * 2048:(pair + 1) * 2048], in_=o[:])
+
+        def mul(dst, a, b2):
+            nc.vector.tensor_tensor(out=dst, in0=a, in1=b2, op=MULT)
+
+        def vector_part(b, cosines, sines):
+            def filler(step):
+                if b > 0:
+                    interleave(b - 1, step)
+
+            p1 = work.tile([P, 512], F32, name="p1_%d" % b, tag="p1")
+            p2 = work.tile([P, 256], F32, name="p2_%d" % b, tag="p2")
+            p3 = work.tile([P, 128], F32, name="p3_%d" % b, tag="p3")
+            r3 = work.tile([P, 128], F32, name="r3_%d" % b, tag="r3")
+            r2 = work.tile([P, 256], F32, name="r2_%d" % b, tag="r2")
+            r1 = work.tile([P, 512], F32, name="r1_%d" % b, tag="r1")
+            num = work.tile([P, 2, 512], F32, name="num_%d" % b, tag="num")
+            mul(p1[:], cosines[:, 0, :], cosines[:, 1, :])
+            mul(num[:], sines[:], cosines[:])
+            mul(p2[:], p1[:, 0:256], p1[:, 256:512])
+            filler(0)
+            mul(p3[:], p2[:, 0:128], p2[:, 128:256])
+            filler(1)
+            nc.vector.reciprocal(out=r3[:], in_=p3[:])
+            filler(2)
+            mul(r2[:, 0:128], r3[:], p2[:, 128:256])
+            mul(r2[:, 128:256], r3[:], p2[:, 0:128])
+            filler(3)
+            mul(r1[:, 0:256], r2[:], p1[:, 256:512])
+            mul(r1[:, 256:512], r2[:], p1[:, 0:256])
+            mul(planes[b][:, :, 3, :], num[:], r1[:].unsqueeze(1).to_broadcast([P, 2, 512]))
+
+        for b in range(BATCHES):
+            cosines, sines = scalar_part(b)
+            vector_part(b, cosines, sines)
+        for step in range(4):
+            interleave(BATCHES - 1, step)

@@ -1,9 +1,7 @@
 import math
 from contextlib import ExitStack
 
-import concourse.bass as bass
 import concourse.mybir as mybir
-import concourse.tile as tile
 from concourse.masks import make_identity
 
 FLOPS = 2 * 2048 * 512 * 1024
@@ -19,7 +17,6 @@ MULT = mybir.AluOpType.mult
 P = 128
 K = 512
 ROW_TILES = 16
-PAIRS = 8
 BATCHES = 4
 
 
@@ -29,24 +26,39 @@ def tile_mylayerfunc_kernel(tc, x, weight, out):
         keep = ctx.enter_context(tc.tile_pool(name="keep", bufs=1))
         work = ctx.enter_context(tc.tile_pool(name="work", bufs=2))
         psum = ctx.enter_context(tc.psum_pool(name="psum", bufs=8))
+        ctx.enter_context(tc.manual_schedule())
 
-        half_pi = keep.tile([P, 1], F32, name="half_pi")
         zero = keep.tile([P, 1], F32, name="zero")
+        half_pi = keep.tile([P, 1], F32, name="half_pi")
+        warm = keep.tile([P, 1], F32, name="warm")
+        ident = keep.tile([P, P], F32, name="ident")
         nc.vector.memset(zero[:], 0.0)
         nc.vector.tensor_scalar_add(out=half_pi[:], in0=zero[:], scalar1=math.pi / 2)
-        warm = keep.tile([P, 1], F32, name="warm")
         nc.scalar.activation(out=warm[:], in_=half_pi[:], func=ACT.Sin)
-        ident = keep.tile([P, P], F32, name="ident")
         make_identity(nc, ident[:])
 
-        w_raw = keep.tile([P, 2 * 4 * K], BF16, name="w_raw")
-        w_view = weight.rearrange("(h p c) k -> h p (c k)", h=2, p=P, c=4)
-        for h in range(2):
-            nc.sync.dma_start(out=w_raw[:, h * 2048:(h + 1) * 2048], in_=w_view[h])
+        w_raw = keep.tile([P, 4 * 2 * K], BF16, name="w_raw")
         x_raw = keep.tile([P, ROW_TILES * K], BF16, name="x_raw")
+        w_view = weight.rearrange("(h p c) k -> c p h k", h=2, p=P, c=4)
         x_view = x.rearrange("(p r) k -> p (r k)", r=ROW_TILES)
-        for b in range(BATCHES):
-            nc.sync.dma_start(out=x_raw[:, b * 2048:(b + 1) * 2048], in_=x_view[:, b * 2048:(b + 1) * 2048])
+
+        def load_w(c):
+            nc.sync.dma_start(
+                out=w_raw[:, c * 1024:(c + 1) * 1024].rearrange("p (h k) -> p h k", h=2), in_=w_view[c]
+            )
+
+        def load_x(lo, hi):
+            nc.sync.dma_start(out=x_raw[:, lo * K:hi * K], in_=x_view[:, lo * K:hi * K])
+
+        load_w(3)
+        load_x(0, 2)
+        load_x(2, 4)
+        load_x(4, 8)
+        load_w(1)
+        load_w(2)
+        load_w(0)
+        load_x(8, 12)
+        load_x(12, 16)
         w_words = w_raw[:].bitcast(F32)
         x_words = x_raw[:].bitcast(F32)
 
@@ -59,12 +71,12 @@ def tile_mylayerfunc_kernel(tc, x, weight, out):
         x_codes = keep.tile([P, 2048], U32, name="x_codes", align_bytes=64)
         x_scales = keep.tile([P, 2048], U8, name="x_scales", align_bytes=64)
 
-        def transpose_bank(words, starts, label):
+        def transpose_bank(words, first, label):
             bank = psum.tile([P, 512], F32, name=label, tag="bank")
             halves = bank[:].rearrange("p (u n) -> p u n", u=2)
             for blk in range(2):
                 for u in range(2):
-                    lo = starts[blk] + u * P
+                    lo = first + blk * 256 + u * P
                     nc.tensor.transpose(halves[:, u, blk * P:(blk + 1) * P], words[:, lo:lo + P], ident[:])
             return bank
 
@@ -76,37 +88,36 @@ def tile_mylayerfunc_kernel(tc, x, weight, out):
             else:
                 nc.scalar.copy(out=dst, in_=src)
 
-        w_banks = [transpose_bank(w_words, [c * 256, 1024 + c * 256], "wt%d" % c) for c in range(4)]
-        for c in range(4):
-            leave(c % 2 == 0, w_banks[c], w_grp_words[:, c * 512:(c + 1) * 512])
-        x_banks = {}
-        for q in range(4):
-            x_banks[q] = transpose_bank(x_words, [2 * q * 256, (2 * q + 1) * 256], "xt%d" % q)
-        for c in range(4):
+        wt = {}
+        xt = {}
+
+        def tw(c):
+            wt[c] = transpose_bank(w_words, c * 512, "wt%d" % c)
+
+        def tx(q):
+            xt[q] = transpose_bank(x_words, q * 512, "xt%d" % q)
+
+        def ew(c, on_vector):
+            leave(on_vector, wt[c], w_grp_words[:, c * 512:(c + 1) * 512])
+
+        def ex(q, on_vector):
+            leave(on_vector, xt[q], x_grp_words[:, q * 512:(q + 1) * 512])
+
+        def qw(c):
             nc.vector.quantize_mx(
                 out=w_codes[:, c * 256:(c + 1) * 256].bitcast(FP8X4),
                 scales=w_scales[:, c * 256:(c + 1) * 256],
                 in_=w_grp[:, c * 1024:(c + 1) * 1024],
             )
-            leave(c % 2 == 0, x_banks[c], x_grp_words[:, c * 512:(c + 1) * 512])
-        for q in range(4, PAIRS):
-            x_banks[q] = transpose_bank(x_words, [2 * q * 256, (2 * q + 1) * 256], "xt%d" % q)
 
-        def quantise_x(b):
+        def qx(first_pair, pairs):
+            lo = first_pair * 256
+            hi = (first_pair + pairs) * 256
             nc.vector.quantize_mx(
-                out=x_codes[:, b * 512:(b + 1) * 512].bitcast(FP8X4),
-                scales=x_scales[:, b * 512:(b + 1) * 512],
-                in_=x_grp[:, b * 2048:(b + 1) * 2048],
+                out=x_codes[:, lo:hi].bitcast(FP8X4),
+                scales=x_scales[:, lo:hi],
+                in_=x_grp[:, 4 * lo:4 * hi],
             )
-
-        quantise_x(0)
-        leave(True, x_banks[4], x_grp_words[:, 4 * 512:5 * 512])
-        leave(False, x_banks[5], x_grp_words[:, 5 * 512:6 * 512])
-        quantise_x(1)
-        leave(True, x_banks[6], x_grp_words[:, 6 * 512:7 * 512])
-        leave(False, x_banks[7], x_grp_words[:, 7 * 512:8 * 512])
-        quantise_x(2)
-        quantise_x(3)
 
         def mx_bank(pair, cls):
             bank = psum.tile([P, 512], F32, name="y%d_%d" % (cls, pair), tag="bank")
@@ -124,38 +135,43 @@ def tile_mylayerfunc_kernel(tc, x, weight, out):
             return bank
 
         out_view = out.rearrange("(p r) j -> p (r j)", r=ROW_TILES)
-        planes = {}
-
-        def scalar_part(b):
-            cosines = work.tile([P, 2, 512], F32, name="cos3_%d" % b, tag="cos3")
-            sines = work.tile([P, 2, 512], F32, name="sin3_%d" % b, tag="sin3")
-            mags = work.tile([P, 2, 512], F32, name="abs3_%d" % b, tag="abs3")
-            res = work.tile([P, 2, 4, 512], F32, name="res_%d" % b, tag="res", bufs=3)
-            pa = 2 * b
-            pb = 2 * b + 1
-            y3a = mx_bank(pa, 3)
-            y3b = mx_bank(pb, 3)
-            nc.scalar.activation(out=mags[:, 0, :], in_=y3a[:], func=ACT.Abs)
-            nc.scalar.activation(out=sines[:, 1, :], in_=y3a[:], func=ACT.Sin)
-            nc.scalar.activation(out=mags[:, 1, :], in_=y3b[:], func=ACT.Abs)
-            nc.scalar.activation(out=cosines[:, 0, :], in_=mags[:, 0, :], func=ACT.Sin, scale=-1.0, bias=half_pi[:])
-            nc.scalar.activation(out=sines[:, 0, :], in_=y3b[:], func=ACT.Sin)
-            nc.scalar.activation(out=cosines[:, 1, :], in_=mags[:, 1, :], func=ACT.Sin, scale=-1.0, bias=half_pi[:])
-            for pair, slot in ((pa, 1), (pb, 0)):
-                mag1 = work.tile([P, 512], F32, name="abs1_%d" % pair, tag="abs1")
-                y1 = mx_bank(pair, 1)
-                y2 = mx_bank(pair, 2)
-                y0 = mx_bank(pair, 0)
-                nc.scalar.activation(out=mag1[:], in_=y1[:], func=ACT.Abs)
-                nc.scalar.activation(out=res[:, slot, 2, :], in_=y2[:], func=ACT.Sin)
-                nc.scalar.activation(out=res[:, slot, 1, :], in_=mag1[:], func=ACT.Sin, scale=-1.0, bias=half_pi[:])
-                nc.scalar.copy(out=res[:, slot, 0, :], in_=y0[:])
-            planes[b] = res
-            return cosines, sines
-
+        y3 = {}
+        rest = {}
+        cos3 = {}
+        sin3 = {}
+        res = {}
         stage = {}
 
-        def interleave(b, step):
+        def mx_tan(pair):
+            y3[pair] = mx_bank(pair, 3)
+
+        def mx_rest(pair):
+            rest[pair] = [mx_bank(pair, 1), mx_bank(pair, 2), mx_bank(pair, 0)]
+
+        def tan_scalar(b):
+            cos3[b] = work.tile([P, 2, 512], F32, name="cos3_%d" % b, tag="cos3")
+            sin3[b] = work.tile([P, 2, 512], F32, name="sin3_%d" % b, tag="sin3")
+            res[b] = work.tile([P, 2, 4, 512], F32, name="res_%d" % b, tag="res", bufs=3)
+            mags = work.tile([P, 2, 512], F32, name="abs3_%d" % b, tag="abs3")
+            ya = y3[2 * b]
+            yb = y3[2 * b + 1]
+            nc.scalar.activation(out=mags[:, 0, :], in_=ya[:], func=ACT.Abs)
+            nc.scalar.activation(out=sin3[b][:, 1, :], in_=ya[:], func=ACT.Sin)
+            nc.scalar.activation(out=mags[:, 1, :], in_=yb[:], func=ACT.Abs)
+            nc.scalar.activation(out=sin3[b][:, 0, :], in_=yb[:], func=ACT.Sin)
+            nc.scalar.activation(out=cos3[b][:], in_=mags[:], func=ACT.Sin, scale=-1.0, bias=half_pi[:])
+
+        def rest_scalar(pair):
+            b = pair // 2
+            slot = 1 - pair % 2
+            y1, y2, y0 = rest[pair]
+            mag1 = work.tile([P, 512], F32, name="abs1_%d" % pair, tag="abs1")
+            nc.scalar.activation(out=mag1[:], in_=y1[:], func=ACT.Abs)
+            nc.scalar.activation(out=res[b][:, slot, 2, :], in_=y2[:], func=ACT.Sin)
+            nc.scalar.activation(out=res[b][:, slot, 1, :], in_=mag1[:], func=ACT.Sin, scale=-1.0, bias=half_pi[:])
+            nc.scalar.copy(out=res[b][:, slot, 0, :], in_=y0[:])
+
+        def interleave(b, step, fine):
             j = step // 2
             t = step % 2
             pair = 2 * b + j
@@ -165,19 +181,24 @@ def tile_mylayerfunc_kernel(tc, x, weight, out):
             o = stage[pair]
             nc.vector.tensor_copy(
                 out=o[:, t * 1024:(t + 1) * 1024].rearrange("p (i c) -> p i c", c=4),
-                in_=planes[b][:, slot, :, t * 256:(t + 1) * 256].rearrange("p c i -> p i c"),
+                in_=res[b][:, slot, :, t * 256:(t + 1) * 256].rearrange("p c i -> p i c"),
             )
-            if t == 1:
+            if fine:
+                r = 2 * pair + t
+                nc.sync.dma_start(out=out_view[:, r * 1024:(r + 1) * 1024], in_=o[:, t * 1024:(t + 1) * 1024])
+            elif t == 1:
                 nc.sync.dma_start(out=out_view[:, pair * 2048:(pair + 1) * 2048], in_=o[:])
 
         def mul(dst, a, b2):
             nc.vector.tensor_tensor(out=dst, in0=a, in1=b2, op=MULT)
 
-        def vector_part(b, cosines, sines):
-            def filler(step):
-                if b > 0:
-                    interleave(b - 1, step)
+        def chain(b, fill):
+            def gap(i):
+                if fill[i] is not None:
+                    fill[i]()
 
+            cs = cos3[b]
+            sn = sin3[b]
             p1 = work.tile([P, 512], F32, name="p1_%d" % b, tag="p1")
             p2 = work.tile([P, 256], F32, name="p2_%d" % b, tag="p2")
             p3 = work.tile([P, 128], F32, name="p3_%d" % b, tag="p3")
@@ -185,23 +206,72 @@ def tile_mylayerfunc_kernel(tc, x, weight, out):
             r2 = work.tile([P, 256], F32, name="r2_%d" % b, tag="r2")
             r1 = work.tile([P, 512], F32, name="r1_%d" % b, tag="r1")
             num = work.tile([P, 2, 512], F32, name="num_%d" % b, tag="num")
-            mul(p1[:], cosines[:, 0, :], cosines[:, 1, :])
-            mul(num[:], sines[:], cosines[:])
+            mul(p1[:], cs[:, 0, :], cs[:, 1, :])
+            mul(num[:, 0, :], sn[:, 0, :], cs[:, 0, :])
             mul(p2[:], p1[:, 0:256], p1[:, 256:512])
-            filler(0)
+            mul(num[:, 1, :], sn[:, 1, :], cs[:, 1, :])
             mul(p3[:], p2[:, 0:128], p2[:, 128:256])
-            filler(1)
+            gap(0)
             nc.vector.reciprocal(out=r3[:], in_=p3[:])
-            filler(2)
+            gap(1)
             mul(r2[:, 0:128], r3[:], p2[:, 128:256])
             mul(r2[:, 128:256], r3[:], p2[:, 0:128])
-            filler(3)
+            gap(2)
             mul(r1[:, 0:256], r2[:], p1[:, 256:512])
             mul(r1[:, 256:512], r2[:], p1[:, 0:256])
-            mul(planes[b][:, :, 3, :], num[:], r1[:].unsqueeze(1).to_broadcast([P, 2, 512]))
+            gap(3)
+            mul(res[b][:, :, 3, :], num[:], r1[:].unsqueeze(1).to_broadcast([P, 2, 512]))
+            gap(4)
 
+        def weave(b, first):
+            return [first] + [lambda s=s: interleave(b, s, False) for s in range(4)]
+
+        tw(3)
+        tx(0)
+        tx(1)
+        ew(3, False)
+        ex(0, True)
+        qw(3)
+        qx(0, 1)
+        mx_tan(0)
+        tx(2)
+        tx(3)
+        ex(1, True)
+        ex(2, True)
+        qx(1, 1)
+        mx_tan(1)
+        tw(1)
+        tw(2)
+        tw(0)
+        tan_scalar(0)
+        ex(3, True)
+        ew(1, True)
+        qx(2, 2)
+        mx_tan(2)
+        mx_tan(3)
+        ew(2, False)
+        ew(0, False)
+        qw(1)
+        chain(0, [lambda: qw(2), lambda: qw(0), None, None, None])
         for b in range(BATCHES):
-            cosines, sines = scalar_part(b)
-            vector_part(b, cosines, sines)
+            nxt = b + 1
+            if nxt < BATCHES:
+                tan_scalar(nxt)
+            if nxt + 1 < BATCHES:
+                tx(2 * nxt + 2)
+                tx(2 * nxt + 3)
+                ex(2 * nxt + 2, False)
+                ex(2 * nxt + 3, False)
+            mx_rest(2 * b)
+            mx_rest(2 * b + 1)
+            rest_scalar(2 * b)
+            rest_scalar(2 * b + 1)
+            if nxt < BATCHES:
+                if nxt + 1 < BATCHES:
+                    chain(nxt, weave(b, lambda n=nxt: qx(2 * n + 2, 2)))
+                    mx_tan(2 * nxt + 2)
+                    mx_tan(2 * nxt + 3)
+                else:
+                    chain(nxt, weave(b, None))
         for step in range(4):
-            interleave(BATCHES - 1, step)
+            interleave(BATCHES - 1, step, True)

@@ -180,8 +180,8 @@ def tile_mylayerfunc_kernel(tc, x, weight, out):
                 stage[pair] = work.tile([P, 2048], F32, name="o_%d" % pair, tag="o", bufs=4)
             o = stage[pair]
             nc.vector.tensor_copy(
-                out=o[:, t * 1024:(t + 1) * 1024].rearrange("p (i c) -> p i c", c=4),
-                in_=res[b][:, slot, :, t * 256:(t + 1) * 256].rearrange("p c i -> p i c"),
+                out=o[:, t * 1024:(t + 1) * 1024].rearrange("p (g i c) -> p g c i", i=4, c=4),
+                in_=res[b][:, slot, :, t * 256:(t + 1) * 256].rearrange("p c (g i) -> p g c i", i=4),
             )
             if fine:
                 r = 2 * pair + t

@@ -224,13 +224,13 @@ def tile_mylayerfunc_kernel(tc, x, weight, out):
             gap(4)
 
         def weave(b, first):
-            return [first] + [lambda s=s: interleave(b, s, False) for s in range(4)]
+            return [first] + [lambda s=s: interleave(b, s, True) for s in range(4)]
 
         tw(3)
         tx(0)
         tx(1)
-        ew(3, False)
-        ex(0, True)
+        ew(3, True)
+        ex(0, False)
         qw(3)
         qx(0, 1)
         mx_tan(0)

@@ -222,9 +222,10 @@ def tile_mylayerfunc_kernel(tc, x, weight, out):
             gap(3)
             mul(res[b][:, :, 3, :], num[:], r1[:].unsqueeze(1).to_broadcast([P, 2, 512]))
             gap(4)
+            gap(5)
 
-        def weave(b, first):
-            return [first] + [lambda s=s: interleave(b, s, True) for s in range(4)]
+        def weave(b, first, last):
+            return [first] + [lambda s=s: interleave(b, s, True) for s in range(4)] + [last]
 
         tw(3)
         tx(0)
@@ -249,29 +250,34 @@ def tile_mylayerfunc_kernel(tc, x, weight, out):
         qx(2, 2)
         mx_tan(2)
         mx_tan(3)
+        tx(4)
+        tx(5)
         ew(2, False)
-        ew(0, False)
         qw(1)
-        chain(0, [lambda: qw(2), lambda: qw(0), None, None, None])
+        chain(0, [lambda: qw(2), lambda: ew(0, True), lambda: qw(0), lambda: ex(4, True), None, None])
         for b in range(BATCHES):
             nxt = b + 1
             if nxt < BATCHES:
                 tan_scalar(nxt)
             if nxt + 1 < BATCHES:
-                tx(2 * nxt + 2)
-                tx(2 * nxt + 3)
-                ex(2 * nxt + 2, False)
                 ex(2 * nxt + 3, False)
             mx_rest(2 * b)
             mx_rest(2 * b + 1)
+            if nxt + 2 < BATCHES:
+                tx(2 * nxt + 4)
+                tx(2 * nxt + 5)
             rest_scalar(2 * b)
             rest_scalar(2 * b + 1)
             if nxt < BATCHES:
+                quantise_next = None
+                leave_next = None
                 if nxt + 1 < BATCHES:
-                    chain(nxt, weave(b, lambda n=nxt: qx(2 * n + 2, 2)))
+                    quantise_next = lambda n=nxt: qx(2 * n + 2, 2)
+                if nxt + 2 < BATCHES:
+                    leave_next = lambda n=nxt: ex(2 * n + 4, True)
+                chain(nxt, weave(b, quantise_next, leave_next))
+                if nxt + 1 < BATCHES:
                     mx_tan(2 * nxt + 2)
                     mx_tan(2 * nxt + 3)
-                else:
-                    chain(nxt, weave(b, None))
         for step in range(4):
             interleave(BATCHES - 1, step, True)

@@ -26,7 +26,6 @@ def tile_mylayerfunc_kernel(tc, x, weight, out):
         keep = ctx.enter_context(tc.tile_pool(name="keep", bufs=1))
         work = ctx.enter_context(tc.tile_pool(name="work", bufs=2))
         psum = ctx.enter_context(tc.psum_pool(name="psum", bufs=8))
-        ctx.enter_context(tc.manual_schedule())
 
         zero = keep.tile([P, 1], F32, name="zero")
         half_pi = keep.tile([P, 1], F32, name="half_pi")
@@ -222,10 +221,9 @@ def tile_mylayerfunc_kernel(tc, x, weight, out):
             gap(3)
             mul(res[b][:, :, 3, :], num[:], r1[:].unsqueeze(1).to_broadcast([P, 2, 512]))
             gap(4)
-            gap(5)
 
-        def weave(b, first, last):
-            return [first] + [lambda s=s: interleave(b, s, True) for s in range(4)] + [last]
+        def weave(b, first):
+            return [first] + [lambda s=s: interleave(b, s, True) for s in range(4)]
 
         tw(3)
         tx(0)
@@ -250,34 +248,29 @@ def tile_mylayerfunc_kernel(tc, x, weight, out):
         qx(2, 2)
         mx_tan(2)
         mx_tan(3)
-        tx(4)
-        tx(5)
         ew(2, False)
+        ew(0, False)
         qw(1)
-        chain(0, [lambda: qw(2), lambda: ew(0, True), lambda: qw(0), lambda: ex(4, True), None, None])
+        chain(0, [lambda: qw(2), lambda: qw(0), None, None, None])
         for b in range(BATCHES):
             nxt = b + 1
             if nxt < BATCHES:
                 tan_scalar(nxt)
             if nxt + 1 < BATCHES:
+                tx(2 * nxt + 2)
+                tx(2 * nxt + 3)
+                ex(2 * nxt + 2, False)
                 ex(2 * nxt + 3, False)
             mx_rest(2 * b)
             mx_rest(2 * b + 1)
-            if nxt + 2 < BATCHES:
-                tx(2 * nxt + 4)
-                tx(2 * nxt + 5)
             rest_scalar(2 * b)
             rest_scalar(2 * b + 1)
             if nxt < BATCHES:
-                quantise_next = None
-                leave_next = None
                 if nxt + 1 < BATCHES:
-                    quantise_next = lambda n=nxt: qx(2 * n + 2, 2)
-                if nxt + 2 < BATCHES:
-                    leave_next = lambda n=nxt: ex(2 * n + 4, True)
-                chain(nxt, weave(b, quantise_next, leave_next))
-                if nxt + 1 < BATCHES:
+                    chain(nxt, weave(b, lambda n=nxt: qx(2 * n + 2, 2)))
                     mx_tan(2 * nxt + 2)
                     mx_tan(2 * nxt + 3)
+                else:
+                    chain(nxt, weave(b, None))
         for step in range(4):
             interleave(BATCHES - 1, step, True)

@@ -16,8 +16,20 @@ MULT = mybir.AluOpType.mult
 
 P = 128
 K = 512
+ROW_WORDS = K // 2
+PACK = 4
 ROW_TILES = 16
 BATCHES = 4
+LINEAR = 0
+COS = 1
+SIN = 2
+TAN = 3
+CLASSES = 4
+CLASS_COLS = 256
+OUT_COLS = CLASSES * CLASS_COLS
+PLANE = 2 * CLASS_COLS
+BANK = 512
+assert PLANE == BANK
 
 
 def tile_mylayerfunc_kernel(tc, x, weight, out):
@@ -36,50 +48,52 @@ def tile_mylayerfunc_kernel(tc, x, weight, out):
         nc.scalar.activation(out=warm[:], in_=half_pi[:], func=ACT.Sin)
         make_identity(nc, ident[:])
 
-        w_raw = keep.tile([P, 4 * 2 * K], BF16, name="w_raw")
+        w_raw = keep.tile([P, CLASSES * 2 * K], BF16, name="w_raw")
         x_raw = keep.tile([P, ROW_TILES * K], BF16, name="x_raw")
-        w_view = weight.rearrange("(h p c) k -> c p h k", h=2, p=P, c=4)
+        w_view = weight.rearrange("(h p c) k -> c p h k", h=2, p=P, c=CLASSES)
         x_view = x.rearrange("(p r) k -> p (r k)", r=ROW_TILES)
 
-        def load_w(c):
+        def load_weight(c):
             nc.sync.dma_start(
-                out=w_raw[:, c * 1024:(c + 1) * 1024].rearrange("p (h k) -> p h k", h=2), in_=w_view[c]
+                out=w_raw[:, c * 2 * K:(c + 1) * 2 * K].rearrange("p (h k) -> p h k", h=2), in_=w_view[c]
             )
 
-        def load_x(lo, hi):
-            nc.sync.dma_start(out=x_raw[:, lo * K:hi * K], in_=x_view[:, lo * K:hi * K])
+        def load_x(first_tile, end_tile):
+            nc.sync.dma_start(
+                out=x_raw[:, first_tile * K:end_tile * K], in_=x_view[:, first_tile * K:end_tile * K]
+            )
 
-        load_w(3)
+        load_weight(TAN)
         load_x(0, 2)
         load_x(2, 4)
         load_x(4, 8)
-        load_w(1)
-        load_w(2)
-        load_w(0)
+        load_weight(COS)
+        load_weight(SIN)
+        load_weight(LINEAR)
         load_x(8, 12)
         load_x(12, 16)
         w_words = w_raw[:].bitcast(F32)
         x_words = x_raw[:].bitcast(F32)
 
-        w_grp = keep.tile([P, 4096], BF16, name="w_grp", align_bytes=64)
-        x_grp = keep.tile([P, 8192], BF16, name="x_grp", align_bytes=64)
+        w_grp = keep.tile([P, OUT_COLS * PACK], BF16, name="w_grp", align_bytes=64)
+        x_grp = keep.tile([P, ROW_TILES * P * PACK], BF16, name="x_grp", align_bytes=64)
         w_grp_words = w_grp[:].bitcast(F32)
         x_grp_words = x_grp[:].bitcast(F32)
-        w_codes = keep.tile([P, 1024], U32, name="w_codes", align_bytes=64)
-        w_scales = keep.tile([P, 1024], U8, name="w_scales", align_bytes=64)
-        x_codes = keep.tile([P, 2048], U32, name="x_codes", align_bytes=64)
-        x_scales = keep.tile([P, 2048], U8, name="x_scales", align_bytes=64)
+        w_codes = keep.tile([P, OUT_COLS], U32, name="w_codes", align_bytes=64)
+        w_scales = keep.tile([P, OUT_COLS], U8, name="w_scales", align_bytes=64)
+        x_codes = keep.tile([P, ROW_TILES * P], U32, name="x_codes", align_bytes=64)
+        x_scales = keep.tile([P, ROW_TILES * P], U8, name="x_scales", align_bytes=64)
 
-        def transpose_bank(words, first, label):
-            bank = psum.tile([P, 512], F32, name=label, tag="bank")
+        def transpose_to_bank(words, first_word, label):
+            bank = psum.tile([P, BANK], F32, name=label, tag="bank")
             halves = bank[:].rearrange("p (u n) -> p u n", u=2)
             for blk in range(2):
                 for u in range(2):
-                    lo = first + blk * 256 + u * P
+                    lo = first_word + blk * ROW_WORDS + u * P
                     nc.tensor.transpose(halves[:, u, blk * P:(blk + 1) * P], words[:, lo:lo + P], ident[:])
             return bank
 
-        def leave(on_vector, bank, dst_words):
+        def regroup(on_vector, bank, dst_words):
             dst = dst_words.rearrange("p (n u) -> p n u", u=2)
             src = bank[:].rearrange("p (u n) -> p n u", u=2)
             if on_vector:
@@ -87,190 +101,180 @@ def tile_mylayerfunc_kernel(tc, x, weight, out):
             else:
                 nc.scalar.copy(out=dst, in_=src)
 
-        wt = {}
-        xt = {}
+        w_banks = {}
+        x_banks = {}
 
-        def tw(c):
-            wt[c] = transpose_bank(w_words, c * 512, "wt%d" % c)
+        def transpose_weight(c):
+            w_banks[c] = transpose_to_bank(w_words, c * 2 * ROW_WORDS, "wt%d" % c)
 
-        def tx(q):
-            xt[q] = transpose_bank(x_words, q * 512, "xt%d" % q)
+        def transpose_x(q):
+            x_banks[q] = transpose_to_bank(x_words, q * 2 * ROW_WORDS, "xt%d" % q)
 
-        def ew(c, on_vector):
-            leave(on_vector, wt[c], w_grp_words[:, c * 512:(c + 1) * 512])
+        def regroup_weight(c, on_vector):
+            regroup(on_vector, w_banks[c], w_grp_words[:, c * BANK:(c + 1) * BANK])
 
-        def ex(q, on_vector):
-            leave(on_vector, xt[q], x_grp_words[:, q * 512:(q + 1) * 512])
+        def regroup_x(q, on_vector):
+            regroup(on_vector, x_banks[q], x_grp_words[:, q * BANK:(q + 1) * BANK])
 
-        def qw(c):
+        def quantise_weight(c):
             nc.vector.quantize_mx(
-                out=w_codes[:, c * 256:(c + 1) * 256].bitcast(FP8X4),
-                scales=w_scales[:, c * 256:(c + 1) * 256],
-                in_=w_grp[:, c * 1024:(c + 1) * 1024],
+                out=w_codes[:, c * CLASS_COLS:(c + 1) * CLASS_COLS].bitcast(FP8X4),
+                scales=w_scales[:, c * CLASS_COLS:(c + 1) * CLASS_COLS],
+                in_=w_grp[:, c * CLASS_COLS * PACK:(c + 1) * CLASS_COLS * PACK],
             )
 
-        def qx(first_pair, pairs):
-            lo = first_pair * 256
-            hi = (first_pair + pairs) * 256
+        def quantise_x(first_pair, pairs):
+            lo = first_pair * 2 * P
+            hi = (first_pair + pairs) * 2 * P
             nc.vector.quantize_mx(
                 out=x_codes[:, lo:hi].bitcast(FP8X4),
                 scales=x_scales[:, lo:hi],
-                in_=x_grp[:, 4 * lo:4 * hi],
+                in_=x_grp[:, PACK * lo:PACK * hi],
             )
 
-        def mx_bank(pair, cls):
-            bank = psum.tile([P, 512], F32, name="y%d_%d" % (cls, pair), tag="bank")
+        def multiply(q, c):
+            bank = psum.tile([P, BANK], F32, name="y%d_%d" % (c, q), tag="bank")
             for t in range(2):
-                r = 2 * pair + t
+                r = 2 * q + t
                 nc.tensor.matmul_mx(
-                    out=bank[:, t * 256:(t + 1) * 256],
+                    out=bank[:, t * CLASS_COLS:(t + 1) * CLASS_COLS],
                     lhsT=x_codes[:, r * P:(r + 1) * P].bitcast(FP8X4),
                     lhsT_scale=x_scales[:, r * P:(r + 1) * P],
-                    rhs=w_codes[:, cls * 256:(cls + 1) * 256].bitcast(FP8X4),
-                    rhs_scale=w_scales[:, cls * 256:(cls + 1) * 256],
+                    rhs=w_codes[:, c * CLASS_COLS:(c + 1) * CLASS_COLS].bitcast(FP8X4),
+                    rhs_scale=w_scales[:, c * CLASS_COLS:(c + 1) * CLASS_COLS],
                     start=True,
                     stop=True,
                 )
             return bank
 
         out_view = out.rearrange("(p r) j -> p (r j)", r=ROW_TILES)
-        y3 = {}
-        rest = {}
-        cos3 = {}
-        sin3 = {}
-        res = {}
-        stage = {}
+        y_tan = {}
+        y_rest = {}
+        cosines = {}
+        sines = {}
+        planes = {}
+        woven = {}
 
-        def mx_tan(pair):
-            y3[pair] = mx_bank(pair, 3)
+        def multiply_tan(q):
+            y_tan[q] = multiply(q, TAN)
 
-        def mx_rest(pair):
-            rest[pair] = [mx_bank(pair, 1), mx_bank(pair, 2), mx_bank(pair, 0)]
+        def multiply_rest(q):
+            y_rest[q] = [multiply(q, COS), multiply(q, SIN), multiply(q, LINEAR)]
 
-        def tan_scalar(b):
-            cos3[b] = work.tile([P, 2, 512], F32, name="cos3_%d" % b, tag="cos3")
-            sin3[b] = work.tile([P, 2, 512], F32, name="sin3_%d" % b, tag="sin3")
-            res[b] = work.tile([P, 2, 4, 512], F32, name="res_%d" % b, tag="res", bufs=3)
-            mags = work.tile([P, 2, 512], F32, name="abs3_%d" % b, tag="abs3")
-            ya = y3[2 * b]
-            yb = y3[2 * b + 1]
-            nc.scalar.activation(out=mags[:, 0, :], in_=ya[:], func=ACT.Abs)
-            nc.scalar.activation(out=sin3[b][:, 1, :], in_=ya[:], func=ACT.Sin)
-            nc.scalar.activation(out=mags[:, 1, :], in_=yb[:], func=ACT.Abs)
-            nc.scalar.activation(out=sin3[b][:, 0, :], in_=yb[:], func=ACT.Sin)
-            nc.scalar.activation(out=cos3[b][:], in_=mags[:], func=ACT.Sin, scale=-1.0, bias=half_pi[:])
+        def tan_inputs(b):
+            cosines[b] = work.tile([P, 2, PLANE], F32, name="cos3_%d" % b, tag="cos3")
+            sines[b] = work.tile([P, 2, PLANE], F32, name="sin3_%d" % b, tag="sin3")
+            planes[b] = work.tile([P, 2, CLASSES, PLANE], F32, name="res_%d" % b, tag="res", bufs=3)
+            magnitudes = work.tile([P, 2, PLANE], F32, name="abs3_%d" % b, tag="abs3")
+            y_first = y_tan[2 * b]
+            y_second = y_tan[2 * b + 1]
+            nc.scalar.activation(out=magnitudes[:, 0, :], in_=y_first[:], func=ACT.Abs)
+            nc.scalar.activation(out=sines[b][:, 1, :], in_=y_first[:], func=ACT.Sin)
+            nc.scalar.activation(out=magnitudes[:, 1, :], in_=y_second[:], func=ACT.Abs)
+            nc.scalar.activation(out=sines[b][:, 0, :], in_=y_second[:], func=ACT.Sin)
+            nc.scalar.activation(out=cosines[b][:], in_=magnitudes[:], func=ACT.Sin, scale=-1.0, bias=half_pi[:])
 
-        def rest_scalar(pair):
-            b = pair // 2
-            slot = 1 - pair % 2
-            y1, y2, y0 = rest[pair]
-            mag1 = work.tile([P, 512], F32, name="abs1_%d" % pair, tag="abs1")
-            nc.scalar.activation(out=mag1[:], in_=y1[:], func=ACT.Abs)
-            nc.scalar.activation(out=res[b][:, slot, 2, :], in_=y2[:], func=ACT.Sin)
-            nc.scalar.activation(out=res[b][:, slot, 1, :], in_=mag1[:], func=ACT.Sin, scale=-1.0, bias=half_pi[:])
-            nc.scalar.copy(out=res[b][:, slot, 0, :], in_=y0[:])
-
-        def interleave(b, step, fine):
-            j = step // 2
-            t = step % 2
-            pair = 2 * b + j
-            slot = 1 - j
-            if t == 0:
-                stage[pair] = work.tile([P, 2048], F32, name="o_%d" % pair, tag="o", bufs=4)
-            o = stage[pair]
-            nc.vector.tensor_copy(
-                out=o[:, t * 1024:(t + 1) * 1024].rearrange("p (g i c) -> p g c i", i=4, c=4),
-                in_=res[b][:, slot, :, t * 256:(t + 1) * 256].rearrange("p c (g i) -> p g c i", i=4),
+        def other_classes(q):
+            b = q // 2
+            slot = 1 - q % 2
+            y_cos, y_sin, y_linear = y_rest[q]
+            magnitude = work.tile([P, PLANE], F32, name="abs1_%d" % q, tag="abs1")
+            nc.scalar.activation(out=magnitude[:], in_=y_cos[:], func=ACT.Abs)
+            nc.scalar.activation(out=planes[b][:, slot, SIN, :], in_=y_sin[:], func=ACT.Sin)
+            nc.scalar.activation(
+                out=planes[b][:, slot, COS, :], in_=magnitude[:], func=ACT.Sin, scale=-1.0, bias=half_pi[:]
             )
-            if fine:
-                r = 2 * pair + t
-                nc.sync.dma_start(out=out_view[:, r * 1024:(r + 1) * 1024], in_=o[:, t * 1024:(t + 1) * 1024])
-            elif t == 1:
-                nc.sync.dma_start(out=out_view[:, pair * 2048:(pair + 1) * 2048], in_=o[:])
+            nc.scalar.copy(out=planes[b][:, slot, LINEAR, :], in_=y_linear[:])
 
-        def mul(dst, a, b2):
-            nc.vector.tensor_tensor(out=dst, in0=a, in1=b2, op=MULT)
+        def weave_and_store(b, step):
+            q = 2 * b + step // 2
+            t = step % 2
+            slot = 1 - step // 2
+            if t == 0:
+                woven[q] = work.tile([P, 2 * OUT_COLS], F32, name="o_%d" % q, tag="o", bufs=4)
+            rows = woven[q][:, t * OUT_COLS:(t + 1) * OUT_COLS]
+            nc.vector.tensor_copy(
+                out=rows.rearrange("p (g e c) -> p g c e", e=4, c=CLASSES),
+                in_=planes[b][:, slot, :, t * CLASS_COLS:(t + 1) * CLASS_COLS].rearrange("p c (g e) -> p g c e", e=4),
+            )
+            r = 2 * q + t
+            nc.sync.dma_start(out=out_view[:, r * OUT_COLS:(r + 1) * OUT_COLS], in_=rows)
 
-        def chain(b, fill):
-            def gap(i):
-                if fill[i] is not None:
-                    fill[i]()
+        def mul(dst, left, right):
+            nc.vector.tensor_tensor(out=dst, in0=left, in1=right, op=MULT)
 
-            cs = cos3[b]
-            sn = sin3[b]
-            p1 = work.tile([P, 512], F32, name="p1_%d" % b, tag="p1")
-            p2 = work.tile([P, 256], F32, name="p2_%d" % b, tag="p2")
-            p3 = work.tile([P, 128], F32, name="p3_%d" % b, tag="p3")
-            r3 = work.tile([P, 128], F32, name="r3_%d" % b, tag="r3")
-            r2 = work.tile([P, 256], F32, name="r2_%d" % b, tag="r2")
-            r1 = work.tile([P, 512], F32, name="r1_%d" % b, tag="r1")
-            num = work.tile([P, 2, 512], F32, name="num_%d" % b, tag="num")
+        def divide(b):
+            cs = cosines[b]
+            sn = sines[b]
+            half = PLANE // 2
+            quarter = PLANE // 4
+            p1 = work.tile([P, PLANE], F32, name="p1_%d" % b, tag="p1")
+            p2 = work.tile([P, half], F32, name="p2_%d" % b, tag="p2")
+            p3 = work.tile([P, quarter], F32, name="p3_%d" % b, tag="p3")
+            r3 = work.tile([P, quarter], F32, name="r3_%d" % b, tag="r3")
+            r2 = work.tile([P, half], F32, name="r2_%d" % b, tag="r2")
+            r1 = work.tile([P, PLANE], F32, name="r1_%d" % b, tag="r1")
+            num = work.tile([P, 2, PLANE], F32, name="num_%d" % b, tag="num")
             mul(p1[:], cs[:, 0, :], cs[:, 1, :])
             mul(num[:, 0, :], sn[:, 0, :], cs[:, 0, :])
-            mul(p2[:], p1[:, 0:256], p1[:, 256:512])
+            mul(p2[:], p1[:, 0:half], p1[:, half:PLANE])
             mul(num[:, 1, :], sn[:, 1, :], cs[:, 1, :])
-            mul(p3[:], p2[:, 0:128], p2[:, 128:256])
-            gap(0)
+            mul(p3[:], p2[:, 0:quarter], p2[:, quarter:half])
             nc.vector.reciprocal(out=r3[:], in_=p3[:])
-            gap(1)
-            mul(r2[:, 0:128], r3[:], p2[:, 128:256])
-            mul(r2[:, 128:256], r3[:], p2[:, 0:128])
-            gap(2)
-            mul(r1[:, 0:256], r2[:], p1[:, 256:512])
-            mul(r1[:, 256:512], r2[:], p1[:, 0:256])
-            gap(3)
-            mul(res[b][:, :, 3, :], num[:], r1[:].unsqueeze(1).to_broadcast([P, 2, 512]))
-            gap(4)
+            mul(r2[:, 0:quarter], r3[:], p2[:, quarter:half])
+            mul(r2[:, quarter:half], r3[:], p2[:, 0:quarter])
+            mul(r1[:, 0:half], r2[:], p1[:, half:PLANE])
+            mul(r1[:, half:PLANE], r2[:], p1[:, 0:half])
+            mul(planes[b][:, :, TAN, :], num[:], r1[:].unsqueeze(1).to_broadcast([P, 2, PLANE]))
 
-        def weave(b, first):
-            return [first] + [lambda s=s: interleave(b, s, True) for s in range(4)]
+        transpose_weight(TAN)
+        transpose_x(0)
+        transpose_x(1)
+        regroup_weight(TAN, True)
+        regroup_x(0, False)
+        quantise_weight(TAN)
+        quantise_x(0, 1)
+        multiply_tan(0)
+        transpose_x(2)
+        transpose_x(3)
+        regroup_x(1, True)
+        regroup_x(2, True)
+        quantise_x(1, 1)
+        multiply_tan(1)
+        transpose_weight(COS)
+        transpose_weight(SIN)
+        transpose_weight(LINEAR)
+        tan_inputs(0)
+        regroup_x(3, True)
+        regroup_weight(COS, True)
+        quantise_x(2, 2)
+        multiply_tan(2)
+        multiply_tan(3)
+        regroup_weight(SIN, False)
+        regroup_weight(LINEAR, False)
+        quantise_weight(COS)
+        quantise_weight(SIN)
+        quantise_weight(LINEAR)
+        divide(0)
 
-        tw(3)
-        tx(0)
-        tx(1)
-        ew(3, True)
-        ex(0, False)
-        qw(3)
-        qx(0, 1)
-        mx_tan(0)
-        tx(2)
-        tx(3)
-        ex(1, True)
-        ex(2, True)
-        qx(1, 1)
-        mx_tan(1)
-        tw(1)
-        tw(2)
-        tw(0)
-        tan_scalar(0)
-        ex(3, True)
-        ew(1, True)
-        qx(2, 2)
-        mx_tan(2)
-        mx_tan(3)
-        ew(2, False)
-        ew(0, False)
-        qw(1)
-        chain(0, [lambda: qw(2), lambda: qw(0), None, None, None])
         for b in range(BATCHES):
-            nxt = b + 1
-            if nxt < BATCHES:
-                tan_scalar(nxt)
-            if nxt + 1 < BATCHES:
-                tx(2 * nxt + 2)
-                tx(2 * nxt + 3)
-                ex(2 * nxt + 2, False)
-                ex(2 * nxt + 3, False)
-            mx_rest(2 * b)
-            mx_rest(2 * b + 1)
-            rest_scalar(2 * b)
-            rest_scalar(2 * b + 1)
-            if nxt < BATCHES:
-                if nxt + 1 < BATCHES:
-                    chain(nxt, weave(b, lambda n=nxt: qx(2 * n + 2, 2)))
-                    mx_tan(2 * nxt + 2)
-                    mx_tan(2 * nxt + 3)
-                else:
-                    chain(nxt, weave(b, None))
-        for step in range(4):
-            interleave(BATCHES - 1, step, True)
+            ahead = b + 1
+            if ahead < BATCHES:
+                tan_inputs(ahead)
+            if ahead + 1 < BATCHES:
+                transpose_x(2 * ahead + 2)
+                transpose_x(2 * ahead + 3)
+                regroup_x(2 * ahead + 2, False)
+                regroup_x(2 * ahead + 3, False)
+            multiply_rest(2 * b)
+            multiply_rest(2 * b + 1)
+            other_classes(2 * b)
+            other_classes(2 * b + 1)
+            if ahead + 1 < BATCHES:
+                quantise_x(2 * ahead + 2, 2)
+                multiply_tan(2 * ahead + 2)
+                multiply_tan(2 * ahead + 3)
+            if ahead < BATCHES:
+                divide(ahead)
+            for step in range(4):
+                weave_and_store(b, step)

import math
from contextlib import ExitStack

import concourse.mybir as mybir
from concourse.masks import make_identity

FLOPS = 2 * 2048 * 512 * 1024

F32 = mybir.dt.float32
BF16 = mybir.dt.bfloat16
U32 = mybir.dt.uint32
U8 = mybir.dt.uint8
FP8X4 = mybir.dt.float8_e4m3fn_x4
ACT = mybir.ActivationFunctionType
MULT = mybir.AluOpType.mult

P = 128
K = 512
ROW_WORDS = K // 2
PACK = 4
ROW_TILES = 16
BATCHES = 4
LINEAR = 0
COS = 1
SIN = 2
TAN = 3
CLASSES = 4
CLASS_COLS = 256
OUT_COLS = CLASSES * CLASS_COLS
PLANE = 2 * CLASS_COLS
BANK = 512
assert PLANE == BANK


def tile_mylayerfunc_kernel(tc, x, weight, out):
    nc = tc.nc
    with ExitStack() as ctx:
        keep = ctx.enter_context(tc.tile_pool(name="keep", bufs=1))
        work = ctx.enter_context(tc.tile_pool(name="work", bufs=2))
        psum = ctx.enter_context(tc.psum_pool(name="psum", bufs=8))

        zero = keep.tile([P, 1], F32, name="zero")
        half_pi = keep.tile([P, 1], F32, name="half_pi")
        warm = keep.tile([P, 1], F32, name="warm")
        ident = keep.tile([P, P], F32, name="ident")
        nc.vector.memset(zero[:], 0.0)
        nc.vector.tensor_scalar_add(out=half_pi[:], in0=zero[:], scalar1=math.pi / 2)
        nc.scalar.activation(out=warm[:], in_=half_pi[:], func=ACT.Sin)
        make_identity(nc, ident[:])

        w_raw = keep.tile([P, CLASSES * 2 * K], BF16, name="w_raw")
        x_raw = keep.tile([P, ROW_TILES * K], BF16, name="x_raw")
        w_view = weight.rearrange("(h p c) k -> c p h k", h=2, p=P, c=CLASSES)
        x_view = x.rearrange("(p r) k -> p (r k)", r=ROW_TILES)

        def load_weight(c):
            nc.sync.dma_start(
                out=w_raw[:, c * 2 * K:(c + 1) * 2 * K].rearrange("p (h k) -> p h k", h=2), in_=w_view[c]
            )

        def load_x(first_tile, end_tile):
            nc.sync.dma_start(
                out=x_raw[:, first_tile * K:end_tile * K], in_=x_view[:, first_tile * K:end_tile * K]
            )

        load_weight(TAN)
        load_x(0, 2)
        load_x(2, 4)
        load_x(4, 8)
        load_weight(COS)
        load_weight(SIN)
        load_weight(LINEAR)
        load_x(8, 12)
        load_x(12, 16)
        w_words = w_raw[:].bitcast(F32)
        x_words = x_raw[:].bitcast(F32)

        w_grp = keep.tile([P, OUT_COLS * PACK], BF16, name="w_grp", align_bytes=64)
        x_grp = keep.tile([P, ROW_TILES * P * PACK], BF16, name="x_grp", align_bytes=64)
        w_grp_words = w_grp[:].bitcast(F32)
        x_grp_words = x_grp[:].bitcast(F32)
        w_codes = keep.tile([P, OUT_COLS], U32, name="w_codes", align_bytes=64)
        w_scales = keep.tile([P, OUT_COLS], U8, name="w_scales", align_bytes=64)
        x_codes = keep.tile([P, ROW_TILES * P], U32, name="x_codes", align_bytes=64)
        x_scales = keep.tile([P, ROW_TILES * P], U8, name="x_scales", align_bytes=64)

        def transpose_to_bank(words, first_word, label):
            bank = psum.tile([P, BANK], F32, name=label, tag="bank")
            halves = bank[:].rearrange("p (u n) -> p u n", u=2)
            for blk in range(2):
                for u in range(2):
                    lo = first_word + blk * ROW_WORDS + u * P
                    nc.tensor.transpose(halves[:, u, blk * P:(blk + 1) * P], words[:, lo:lo + P], ident[:])
            return bank

        def regroup(on_vector, bank, dst_words):
            dst = dst_words.rearrange("p (n u) -> p n u", u=2)
            src = bank[:].rearrange("p (u n) -> p n u", u=2)
            if on_vector:
                nc.vector.tensor_copy(out=dst, in_=src)
            else:
                nc.scalar.copy(out=dst, in_=src)

        w_banks = {}
        x_banks = {}

        def transpose_weight(c):
            w_banks[c] = transpose_to_bank(w_words, c * 2 * ROW_WORDS, "wt%d" % c)

        def transpose_x(q):
            x_banks[q] = transpose_to_bank(x_words, q * 2 * ROW_WORDS, "xt%d" % q)

        def regroup_weight(c, on_vector):
            regroup(on_vector, w_banks[c], w_grp_words[:, c * BANK:(c + 1) * BANK])

        def regroup_x(q, on_vector):
            regroup(on_vector, x_banks[q], x_grp_words[:, q * BANK:(q + 1) * BANK])

        def quantise_weight(c):
            nc.vector.quantize_mx(
                out=w_codes[:, c * CLASS_COLS:(c + 1) * CLASS_COLS].bitcast(FP8X4),
                scales=w_scales[:, c * CLASS_COLS:(c + 1) * CLASS_COLS],
                in_=w_grp[:, c * CLASS_COLS * PACK:(c + 1) * CLASS_COLS * PACK],
            )

        def quantise_x(first_pair, pairs):
            lo = first_pair * 2 * P
            hi = (first_pair + pairs) * 2 * P
            nc.vector.quantize_mx(
                out=x_codes[:, lo:hi].bitcast(FP8X4),
                scales=x_scales[:, lo:hi],
                in_=x_grp[:, PACK * lo:PACK * hi],
            )

        def multiply(q, c):
            bank = psum.tile([P, BANK], F32, name="y%d_%d" % (c, q), tag="bank")
            for t in range(2):
                r = 2 * q + t
                nc.tensor.matmul_mx(
                    out=bank[:, t * CLASS_COLS:(t + 1) * CLASS_COLS],
                    lhsT=x_codes[:, r * P:(r + 1) * P].bitcast(FP8X4),
                    lhsT_scale=x_scales[:, r * P:(r + 1) * P],
                    rhs=w_codes[:, c * CLASS_COLS:(c + 1) * CLASS_COLS].bitcast(FP8X4),
                    rhs_scale=w_scales[:, c * CLASS_COLS:(c + 1) * CLASS_COLS],
                    start=True,
                    stop=True,
                )
            return bank

        out_view = out.rearrange("(p r) j -> p (r j)", r=ROW_TILES)
        y_tan = {}
        y_rest = {}
        cosines = {}
        sines = {}
        planes = {}
        woven = {}

        def multiply_tan(q):
            y_tan[q] = multiply(q, TAN)

        def multiply_rest(q):
            y_rest[q] = [multiply(q, COS), multiply(q, SIN), multiply(q, LINEAR)]

        def tan_inputs(b):
            cosines[b] = work.tile([P, 2, PLANE], F32, name="cos3_%d" % b, tag="cos3")
            sines[b] = work.tile([P, 2, PLANE], F32, name="sin3_%d" % b, tag="sin3")
            planes[b] = work.tile([P, 2, CLASSES, PLANE], F32, name="res_%d" % b, tag="res", bufs=3)
            magnitudes = work.tile([P, 2, PLANE], F32, name="abs3_%d" % b, tag="abs3")
            y_first = y_tan[2 * b]
            y_second = y_tan[2 * b + 1]
            nc.scalar.activation(out=magnitudes[:, 0, :], in_=y_first[:], func=ACT.Abs)
            nc.scalar.activation(out=sines[b][:, 1, :], in_=y_first[:], func=ACT.Sin)
            nc.scalar.activation(out=magnitudes[:, 1, :], in_=y_second[:], func=ACT.Abs)
            nc.scalar.activation(out=sines[b][:, 0, :], in_=y_second[:], func=ACT.Sin)
            nc.scalar.activation(out=cosines[b][:], in_=magnitudes[:], func=ACT.Sin, scale=-1.0, bias=half_pi[:])

        def other_classes(q):
            b = q // 2
            slot = 1 - q % 2
            y_cos, y_sin, y_linear = y_rest[q]
            magnitude = work.tile([P, PLANE], F32, name="abs1_%d" % q, tag="abs1")
            nc.scalar.activation(out=magnitude[:], in_=y_cos[:], func=ACT.Abs)
            nc.scalar.activation(out=planes[b][:, slot, SIN, :], in_=y_sin[:], func=ACT.Sin)
            nc.scalar.activation(
                out=planes[b][:, slot, COS, :], in_=magnitude[:], func=ACT.Sin, scale=-1.0, bias=half_pi[:]
            )
            nc.scalar.copy(out=planes[b][:, slot, LINEAR, :], in_=y_linear[:])

        def weave_and_store(b, step):
            q = 2 * b + step // 2
            t = step % 2
            slot = 1 - step // 2
            if t == 0:
                woven[q] = work.tile([P, 2 * OUT_COLS], F32, name="o_%d" % q, tag="o", bufs=4)
            rows = woven[q][:, t * OUT_COLS:(t + 1) * OUT_COLS]
            nc.vector.tensor_copy(
                out=rows.rearrange("p (g e c) -> p g c e", e=4, c=CLASSES),
                in_=planes[b][:, slot, :, t * CLASS_COLS:(t + 1) * CLASS_COLS].rearrange("p c (g e) -> p g c e", e=4),
            )
            r = 2 * q + t
            nc.sync.dma_start(out=out_view[:, r * OUT_COLS:(r + 1) * OUT_COLS], in_=rows)

        def mul(dst, left, right):
            nc.vector.tensor_tensor(out=dst, in0=left, in1=right, op=MULT)

        def divide(b):
            cs = cosines[b]
            sn = sines[b]
            half = PLANE // 2
            quarter = PLANE // 4
            p1 = work.tile([P, PLANE], F32, name="p1_%d" % b, tag="p1")
            p2 = work.tile([P, half], F32, name="p2_%d" % b, tag="p2")
            p3 = work.tile([P, quarter], F32, name="p3_%d" % b, tag="p3")
            r3 = work.tile([P, quarter], F32, name="r3_%d" % b, tag="r3")
            r2 = work.tile([P, half], F32, name="r2_%d" % b, tag="r2")
            r1 = work.tile([P, PLANE], F32, name="r1_%d" % b, tag="r1")
            num = work.tile([P, 2, PLANE], F32, name="num_%d" % b, tag="num")
            mul(p1[:], cs[:, 0, :], cs[:, 1, :])
            mul(num[:, 0, :], sn[:, 0, :], cs[:, 0, :])
            mul(p2[:], p1[:, 0:half], p1[:, half:PLANE])
            mul(num[:, 1, :], sn[:, 1, :], cs[:, 1, :])
            mul(p3[:], p2[:, 0:quarter], p2[:, quarter:half])
            nc.vector.reciprocal(out=r3[:], in_=p3[:])
            mul(r2[:, 0:quarter], r3[:], p2[:, quarter:half])
            mul(r2[:, quarter:half], r3[:], p2[:, 0:quarter])
            mul(r1[:, 0:half], r2[:], p1[:, half:PLANE])
            mul(r1[:, half:PLANE], r2[:], p1[:, 0:half])
            mul(planes[b][:, :, TAN, :], num[:], r1[:].unsqueeze(1).to_broadcast([P, 2, PLANE]))

        transpose_weight(TAN)
        transpose_x(0)
        transpose_x(1)
        regroup_weight(TAN, True)
        regroup_x(0, False)
        quantise_weight(TAN)
        quantise_x(0, 1)
        multiply_tan(0)
        transpose_x(2)
        transpose_x(3)
        regroup_x(1, True)
        regroup_x(2, True)
        quantise_x(1, 1)
        multiply_tan(1)
        transpose_weight(COS)
        transpose_weight(SIN)
        transpose_weight(LINEAR)
        tan_inputs(0)
        regroup_x(3, True)
        regroup_weight(COS, True)
        quantise_x(2, 2)
        multiply_tan(2)
        multiply_tan(3)
        regroup_weight(SIN, False)
        regroup_weight(LINEAR, False)
        quantise_weight(COS)
        quantise_weight(SIN)
        quantise_weight(LINEAR)
        divide(0)

        for b in range(BATCHES):
            ahead = b + 1
            if ahead < BATCHES:
                tan_inputs(ahead)
            if ahead + 1 < BATCHES:
                transpose_x(2 * ahead + 2)
                transpose_x(2 * ahead + 3)
                regroup_x(2 * ahead + 2, False)
                regroup_x(2 * ahead + 3, False)
            multiply_rest(2 * b)
            multiply_rest(2 * b + 1)
            other_classes(2 * b)
            other_classes(2 * b + 1)
            if ahead + 1 < BATCHES:
                quantise_x(2 * ahead + 2, 2)
                multiply_tan(2 * ahead + 2)
                multiply_tan(2 * ahead + 3)
            if ahead < BATCHES:
                divide(ahead)
            for step in range(4):
                weave_and_store(b, step)
